import numpy as np
import ml_dtypes


def mxq(x, axis, fmt="e4m3"):
    dtype, down = {"e4m3": (ml_dtypes.float8_e4m3fn, 7), "e5m2": (ml_dtypes.float8_e5m2, 14)}[fmt]
    v = np.moveaxis(np.asarray(x, np.float32).astype(ml_dtypes.bfloat16).astype(np.float64), axis, -1)
    blocks = v.reshape(v.shape[:-1] + (-1, 32))
    amax = np.abs(blocks).max(-1, keepdims=True)
    byte = np.maximum(np.where(amax > 0, np.frexp(amax)[1] - 1 + 127, 0) - down, 1)
    scale = np.exp2(byte - 127.0)
    codes = (blocks / scale).astype(np.float32).astype(dtype).astype(np.float64)
    return np.moveaxis((codes * scale).reshape(v.shape), -1, axis)


WIDE = False


def mx_kscale(k):
    if not WIDE:
        return np.ones(k)
    levels = np.array([10, -10, 5, -5, 0])
    if k % 512:
        return np.exp2(np.random.permutation(np.resize(levels, k // 32))).repeat(32)
    a = np.empty((k // 512, 16))
    for p in range(k // 512):
        a[p, :8] = np.random.permutation(np.resize(levels, 8))
        for g in range(8):
            far = levels[np.abs(levels - a[p, g]) >= 10]
            a[p, g + 8] = far[np.random.randint(len(far))]
    return np.exp2(a.ravel()).repeat(32)


BF16 = ml_dtypes.bfloat16


def bf(x):
    return np.asarray(x, np.float32).astype(BF16)


def f64(x):
    return np.asarray(x).astype(np.float64)


E2M1 = np.array([0.0, 0.5, 1.0, 1.5, 2.0, 3.0, 4.0, 6.0, -0.0, -0.5, -1.0, -1.5, -2.0, -3.0, -4.0, -6.0])


def pack_weight(w, fmt):
    k, n = w.shape
    w = f64(bf(w)).reshape(k // 32, 32, n)
    amax = np.abs(w).max(1)
    if fmt == "e4m3":
        byte = np.frexp(amax)[1] - 1 + 127 - 7
    else:
        mant, ex = np.frexp(amax / 6.0)
        byte = np.where(mant > 0.5, ex, ex - 1) + 127
    byte = np.clip(np.where(amax > 0, byte, 1), 1, 254)
    scaled = (w * np.exp2(127.0 - byte)[:, None, :]).reshape(k, n).astype(np.float32)
    by_word = np.ascontiguousarray(scaled.reshape(k // 512, 128, 4, n).transpose(0, 1, 3, 2))
    if fmt == "e4m3":
        words = by_word.astype(ml_dtypes.float8_e4m3fn).view(np.uint8)
    else:
        c = by_word.astype(ml_dtypes.float4_e2m1fn).view(np.uint8) & 0xF
        words = c[..., 0::2] | (c[..., 1::2] << 4)
    return np.ascontiguousarray(words), np.ascontiguousarray(byte.astype(np.uint8).reshape(k // 512, 16, n))


def unpack_weight(words, scales, fmt):
    g, p, n, _ = words.shape
    if fmt == "e4m3":
        vals = np.ascontiguousarray(words).view(ml_dtypes.float8_e4m3fn).astype(np.float64)
    else:
        nib = np.empty((g, p, n, 4), np.uint8)
        nib[..., 0::2] = words & 0xF
        nib[..., 1::2] = words >> 4
        vals = E2M1[nib]
    vals = vals * np.repeat(np.exp2(scales.astype(np.float64) - 127.0), 8, axis=1)[..., None]
    return vals.transpose(0, 1, 3, 2).reshape(g * 512, n)
def pack4(w):
    words, scales = pack_weight(w, "e2m1")
    return words.reshape(words.shape[0], 128, -1), scales


def unpack4(words, scales):
    return unpack_weight(words.reshape(words.shape[0], 128, -1, 2), scales, "e2m1")


B, S, E, H, C = 1, 512, 2048, 16, 512
HD = E // H
EPS = 1e-5


def silu(v):
    return v / (1.0 + np.exp(-v))


def draw0():
    s, t = mx_kscale(E), mx_kscale(E)
    spread = np.exp(0.7 * np.random.standard_normal((B, S, H, 1)))
    shift = 0.5 * np.random.standard_normal((B, S, H, 1))
    attn = 1.5 * (np.random.standard_normal((B, S, H, HD)) * spread + shift)
    x = bf(np.random.standard_normal((B, S, E)) * s)
    Wg_words, Wg_scales = pack4(np.random.standard_normal((E, E)) / np.sqrt(E) / s[:, None])
    bg = bf(np.random.standard_normal(E) * 0.2)
    gn_w = bf((1.0 + 0.1 * np.random.standard_normal(E)) * t)
    gn_b = bf(0.1 * np.random.standard_normal(E) * t)
    Wo_words, Wo_scales = pack4(np.random.standard_normal((E, E)) * 1.5 / np.sqrt(E) / t[:, None])
    bo = bf(np.random.standard_normal(E) * 0.1)
    return {"x": x,
            "attn": bf(attn.reshape(B, S, E)),
            "Wg_words": Wg_words,
            "Wg_scales": Wg_scales,
            "bg": bg,
            "gn_w": gn_w,
            "gn_b": gn_b,
            "Wo_words": Wo_words,
            "Wo_scales": Wo_scales,
            "bo": bo}


def core(x, attn, Wg_words, Wg_scales, bg, gn_w, gn_b, Wo_words, Wo_scales, bo):
    g = f64(attn).reshape(B, S, H, HD)
    mu = g.mean(-1, keepdims=True)
    var = g.var(-1, keepdims=True)
    g = (g - mu) / np.sqrt(var + EPS)
    g = g.reshape(B, S, E) * f64(gn_w) + f64(gn_b)
    gate = silu((mxq(f64(x), 2, "e4m3") @ unpack4(Wg_words, Wg_scales)) + f64(bg))
    h = gate * g
    return (mxq(h, 2, "e4m3") @ unpack4(Wo_words, Wo_scales)) + f64(bo)


def e4m3fn_bytes(y):
    return np.clip(np.asarray(y, np.float64), -448.0, 448.0).astype(np.float32).astype(ml_dtypes.float8_e4m3fn).view(np.uint8)


def e4m3fn_values(b):
    return np.asarray(b, np.uint8).view(ml_dtypes.float8_e4m3fn).astype(np.float64)


def setup_inputs():
    d = draw0()
    x0 = np.asarray(d['x']).astype(np.float64)
    s = (np.max(np.abs(x0), axis=(0, 1), keepdims=True) / 448.0).astype(np.float32)
    out = {}
    for k, v in d.items():
        if k == 'x':
            out['x_bytes'] = e4m3fn_bytes(x0 / s.astype(np.float64))
            out['x_scale'] = s
        else:
            out[k] = v
    return out


def reference(x_bytes, x_scale, attn, Wg_words, Wg_scales, bg, gn_w, gn_b, Wo_words, Wo_scales, bo):
    return core(e4m3fn_values(x_bytes) * x_scale.astype(np.float64), attn, Wg_words, Wg_scales, bg, gn_w, gn_b, Wo_words, Wo_scales, bo)

@@ -1,0 +1,650 @@
+from contextlib import ExitStack
+
+import concourse.mybir as mybir
+from concourse.masks import make_identity
+
+F32 = mybir.dt.float32
+BF16 = mybir.dt.bfloat16
+I32 = mybir.dt.int32
+U32 = mybir.dt.uint32
+U8 = mybir.dt.uint8
+FP8 = mybir.dt.float8_e4m3fn
+FP8X4 = mybir.dt.float8_e4m3fn_x4
+FP4X4 = mybir.dt.float4_e2m1fn_x4
+ALU = mybir.AluOpType
+ACT = mybir.ActivationFunctionType
+
+P = 128
+TOK = 512
+E = 2048
+PACK = 4
+KP = P * PACK
+NP = E // KP
+NI = TOK // P
+NJ = E // P
+GRP = 128
+EPS = 1e-5
+RSQRT_MAGIC = 1597463007.0
+FLOPS = 2 * 2 * TOK * E * E
+SWEEP = 6
+HALF = TOK // 2
+SPLIT = (P * SWEEP, E - P * SWEEP)
+
+
+def tile_multiscaleretention_pb_w4_kernel(
+    tc, x_bytes, x_scale, attn, Wg_words, Wg_scales, bg, gn_w, gn_b, Wo_words, Wo_scales, bo, out
+):
+    nc = tc.nc
+    with ExitStack() as ctx:
+        keep = ctx.enter_context(tc.tile_pool(name="keep", bufs=1))
+        work = ctx.enter_context(tc.tile_pool(name="work", bufs=2))
+        psum = ctx.enter_context(tc.psum_pool(name="psum", bufs=1))
+        ctx.enter_context(tc.manual_schedule())
+
+        x_tok = x_bytes.rearrange("o (i p) k -> p (o i) k", p=P)
+        attn_tok = attn.rearrange("o (i p) c -> p (o i) c", p=P)
+        scratch = out.rearrange("o a b -> (o a b)").rearrange("(c n) -> c n", n=TOK)
+
+        xb0 = keep.tile([P, NI, KP], U8, name="xb0", align_bytes=64)
+        xb1 = keep.tile([P, NI, E - KP], U8, name="xb1", align_bytes=64)
+        xs = [keep.tile([P, KP], F32, name="xs%d" % g) for g in range(NP)]
+        wgs = [keep.tile([P, NP, n], U8, name="wgs%d" % k, align_bytes=64) for k, n in enumerate(SPLIT)]
+        wos = keep.tile([P, NP, E], U8, name="wos", align_bytes=64)
+        wg = [
+            [keep.tile([P, 2 * n], U8, name="wg%d%d" % (k, g), align_bytes=64) for g in range(NP)]
+            for k, n in enumerate(SPLIT)
+        ]
+        wo = [keep.tile([P, 2 * E], U8, name="wo%d" % g, align_bytes=64) for g in range(NP)]
+        at = [keep.tile([P, E], BF16, name="at%d" % i) for i in range(NI)]
+        bo_bc = keep.tile([P, E], BF16, name="bo_bc")
+        bg_rows = keep.tile([NJ, P], BF16, name="bg_rows")
+        bg_sq = keep.tile([P, P], F32, name="bg_sq")
+        bg_col = keep.tile([P, NJ], F32, name="bg_col")
+        w_raw = keep.tile([P, NP, PACK], BF16, name="w_raw")
+        b_raw = keep.tile([P, NP, PACK], BF16, name="b_raw")
+        w_col = keep.tile([P, NP, PACK], F32, name="w_col")
+        b_col = keep.tile([P, NP, PACK], F32, name="b_col")
+        ident = keep.tile([P, P], F32, name="ident")
+        warm = keep.tile([P, 1], F32, name="warm")
+        xc = [keep.tile([P, TOK], U32, name="xc%d" % g, align_bytes=64) for g in range(NP)]
+        xcs = [keep.tile([P, TOK], U8, name="xcs%d" % g, align_bytes=64) for g in range(NP)]
+        hc = [[keep.tile([P, HALF], U32, name="hc%d%d" % (h, g), align_bytes=64) for g in range(NP)] for h in range(2)]
+        hcs = [[keep.tile([P, HALF], U8, name="hcs%d%d" % (h, g), align_bytes=64) for g in range(NP)] for h in range(2)]
+        sp = [keep.tile([P, PACK, TOK], F32, name="sp%d" % g) for g in range(NP)]
+        NC = 2 * NJ
+        st, var, yi, y0, rs, nmr = ([] for k in range(6))
+        for k in range(2):
+            st.append(keep.tile([P, NC, 6], F32, name="st%d" % k))
+            var.append(keep.tile([P, NC], F32, name="var%d" % k))
+            yi.append(keep.tile([P, NC], I32, name="yi%d" % k))
+            y0.append(keep.tile([P, NC], I32, name="y0%d" % k))
+            rs.append(keep.tile([P, NC], F32, name="rs%d" % k))
+            nmr.append(keep.tile([P, NC], F32, name="nmr%d" % k))
+        ssum = keep.tile([P, NJ], F32, name="ssum")
+        nmean = keep.tile([P, NC], F32, name="nmean")
+        m2 = keep.tile([P, NJ], F32, name="m2")
+
+        x_scale_row = x_scale.rearrange("o u k -> (o u k)")
+
+        def load_x_scale(g):
+            nc.sync.dma_start(out=xs[g][:], in_=x_scale_row[KP * g : KP * (g + 1)].partition_broadcast(P))
+
+        nc.scalar.dma_start(out=bg_rows[:], in_=bg.rearrange("(j q) -> j q", q=P))
+        nc.scalar.dma_start(out=w_raw[:], in_=gn_w.rearrange("(g p t) -> p g t", p=P, t=PACK))
+        nc.scalar.dma_start(out=b_raw[:], in_=gn_b.rearrange("(g p t) -> p g t", p=P, t=PACK))
+
+        nc.vector.memset(warm[:], 0.0)
+        for k in range(2):
+            nc.vector.memset(wgs[k][:].rearrange("p g n -> p (g n)").bitcast(I32), 0)
+        nc.scalar.activation(warm[:], warm[:], ACT.Silu)
+        make_identity(nc, ident[:])
+        nc.gpsimd.memset(wos[:].rearrange("p g n -> p (g n)").bitcast(I32), 0)
+        nc.gpsimd.memset(bg_sq[:], 0.0)
+        nc.gpsimd.tensor_copy(out=bg_sq[0:NJ, :], in_=bg_rows[:])
+        nc.gpsimd.tensor_copy(out=w_col[:], in_=w_raw[:])
+        nc.gpsimd.tensor_copy(out=b_col[:], in_=b_raw[:])
+
+        def load_scales(plane, scales):
+            view = scales.rearrange("g (q r) n -> r q g n", r=4)
+            for r in range(4):
+                nc.sync.dma_start(out=plane[r:P:32, :, :].bitcast(I32), in_=view[r].bitcast(I32))
+
+        first_cols = (slice(0, SPLIT[0]), slice(SPLIT[0], E))
+
+        def load_wg(k, g):
+            lo, hi = first_cols[k].start, first_cols[k].stop
+            nc.sync.dma_start(out=wg[k][g][:], in_=Wg_words[g][:, 2 * lo : 2 * hi])
+
+        def load_attn(i):
+            nc.sync.dma_start(out=at[i][:], in_=attn_tok[:, i, :])
+
+
+        xd = {}
+        xg = {}
+        xbank = {}
+
+        def dequant(g, i):
+            t = work.tile([P, KP], BF16, name="xd", tag="xd", bufs=8, align_bytes=64)
+            src = xb0[:, i, :] if g == 0 else xb1[:, i, KP * (g - 1) : KP * g]
+            nc.vector.tensor_tensor(out=t[:], in0=src.bitcast(FP8), in1=xs[g][:], op=ALU.mult)
+            xd[g, i] = t
+
+        def turn_x(g, b):
+            bank = psum.tile([P, 2, 2, P], F32, name="tr", tag="tr", bufs=2)
+            for l in range(2):
+                words = xd[g, 2 * b + l][:].bitcast(F32)
+                for u in range(2):
+                    nc.tensor.transpose(bank[:, u, l, :], words[:, u : KP // 2 : 2], ident[:])
+            xbank[g, b] = bank
+
+        def lay_x(g, b):
+            if b == 0:
+                xg[g] = work.tile([P, TOK, PACK], BF16, name="xg", tag="xg", bufs=2, align_bytes=64)
+            half = xg[g][:, 2 * P * b : 2 * P * (b + 1), :]
+            nc.scalar.copy(
+                out=half.bitcast(F32), in_=xbank[g, b][:].rearrange("p u l r -> p (l r) u")
+            )
+
+        def quant_x(g):
+            nc.vector.quantize_mx(
+                out=xc[g][:].bitcast(FP8X4), scales=xcs[g][:], in_=xg[g][:].rearrange("p r t -> p (r t)")
+            )
+
+        acc = {}
+        s_tile = {}
+
+        def gate_mx(j, g):
+            k, c = (0, j) if j < SWEEP else (1, j - SWEEP)
+            if g == 0:
+                acc[j] = psum.tile([P, TOK], F32, name="mx", tag="mx", bufs=SWEEP)
+            nc.tensor.matmul_mx(
+                out=acc[j][:],
+                lhsT=wg[k][g][:, 2 * P * c : 2 * P * (c + 1)].bitcast(FP4X4),
+                lhsT_scale=wgs[k][:, g, P * c : P * (c + 1)],
+                rhs=xc[g][:].bitcast(FP8X4),
+                rhs_scale=xcs[g][:],
+                start=(g == 0),
+                stop=(g == NP - 1),
+            )
+
+        def silu(j):
+            s = work.tile([P, TOK], F32, name="s", tag="s", bufs=8)
+            nc.scalar.activation(s[:], acc[j][:], ACT.Silu, bias=bg_col[:, j : j + 1])
+            s_tile[j] = s
+
+        def store_s(j):
+            g, q = divmod(j, 4)
+            for t in range(PACK):
+                nc.sync.dma_start(out=sp[g][32 * q : 32 * (q + 1), t, :], in_=s_tile[j][t:P:4, :])
+
+        def load_s(g):
+            pass
+
+        gh = {}
+        gT = {}
+        hb = {}
+
+        def channels(g, q):
+            return slice(KP * g + GRP * q, KP * g + GRP * (q + 1))
+
+        def stats(i, g):
+            for q in range(4):
+                c = NJ * (i % 2) + 4 * g + q
+                nc.vector.bn_stats(out=st[i // 2][:, c, :], in_=at[i][:, channels(g, q)])
+
+        def sums(i, g):
+            for q in range(4):
+                c = 4 * g + q
+                junk = work.tile([P, GRP], BF16, name="junk", tag="junk", bufs=2)
+                nc.scalar.activation(junk[:], at[0][:, channels(g, q)], ACT.Identity, accum_out=ssum[:, c : c + 1])
+
+        def squares(i, g):
+            for q in range(4):
+                c = 4 * g + q
+                junk = work.tile([P, GRP], BF16, name="junk", tag="junk", bufs=2)
+                nc.scalar.activation(
+                    junk[:], at[0][:, channels(g, q)], ACT.Square,
+                    bias=nmean[:, c : c + 1], accum_out=m2[:, c : c + 1],
+                )
+
+        def mean0():
+            nc.gpsimd.tensor_scalar(
+                out=nmean[:, 0:NJ], in0=ssum[:], scalar1=-1.0 / GRP, scalar2=0.0, op0=ALU.mult, op1=ALU.add
+            )
+
+        def small(name, n=2 * NJ):
+            return work.tile([P, n], F32, name=name, tag=name + str(n), bufs=2)
+
+        def variance(k):
+            lo = 0
+            if k == 0:
+                lo = NJ
+                nc.gpsimd.tensor_scalar(
+                    out=var[0][:, 0:NJ], in0=m2[:], scalar1=1.0 / GRP, scalar2=EPS, op0=ALU.mult, op1=ALU.add
+                )
+            n = NC - lo
+            me, m2e, mo, m2o = (st[k][:, lo:NC, f] for f in (1, 2, 4, 5))
+            d, dd, v, q = small("d", n), small("dd", n), small("v", n), small("q", n)
+            nc.gpsimd.tensor_tensor(out=d[:], in0=me, in1=mo, op=ALU.subtract)
+            nc.gpsimd.tensor_tensor(out=v[:], in0=m2e, in1=m2o, op=ALU.add)
+            nc.gpsimd.tensor_tensor(out=dd[:], in0=d[:], in1=d[:], op=ALU.mult)
+            nc.gpsimd.tensor_scalar(out=v[:], in0=v[:], scalar1=1.0 / GRP, scalar2=EPS, op0=ALU.mult, op1=ALU.add)
+            nc.gpsimd.tensor_scalar(out=q[:], in0=dd[:], scalar1=0.25, scalar2=0.0, op0=ALU.mult, op1=ALU.add)
+            nc.gpsimd.tensor_tensor(out=var[k][:, lo:NC], in0=v[:], in1=q[:], op=ALU.add)
+
+        def seed(k):
+            nc.vector.tensor_scalar(
+                out=yi[k][:], in0=var[k][:].bitcast(I32), scalar1=1, scalar2=None, op0=ALU.arith_shift_right
+            )
+            nc.vector.tensor_scalar(
+                out=y0[k][:], in0=yi[k][:], scalar1=-1.0, scalar2=RSQRT_MAGIC, op0=ALU.mult, op1=ALU.add
+            )
+
+        def newton(k):
+            y = y0[k][:].bitcast(F32)
+            for step in range(3):
+                a, b = small("na"), small("nb")
+                last = rs[k] if step == 2 else small("ny")
+                nc.gpsimd.tensor_tensor(out=a[:], in0=y, in1=y, op=ALU.mult)
+                nc.gpsimd.tensor_tensor(out=b[:], in0=a[:], in1=var[k][:], op=ALU.mult)
+                nc.gpsimd.tensor_scalar(out=b[:], in0=b[:], scalar1=-0.5, scalar2=1.5, op0=ALU.mult, op1=ALU.add)
+                nc.gpsimd.tensor_tensor(out=last[:], in0=y, in1=b[:], op=ALU.mult)
+                y = last[:]
+            lo = NJ if k == 0 else 0
+            nm = nmean if k == 0 else small("nm")
+            nc.gpsimd.tensor_tensor(out=nm[:, lo:NC], in0=st[k][:, lo:NC, 1], in1=st[k][:, lo:NC, 4], op=ALU.add)
+            nc.gpsimd.tensor_scalar(out=nm[:, lo:NC], in0=nm[:, lo:NC], scalar1=-0.5, scalar2=0.0, op0=ALU.mult, op1=ALU.add)
+            nc.gpsimd.tensor_tensor(out=nmr[k][:], in0=nm[:], in1=rs[k][:], op=ALU.mult)
+
+        def norm(i, g, eng):
+            t = work.tile([P, PACK, P], F32, name="gh", tag="gh", bufs=10)
+            for q in range(4):
+                c = NJ * (i % 2) + 4 * g + q
+                src = at[i][:, channels(g, q)].rearrange("p (m t) -> p t m", t=PACK)
+                dst = t[:, :, 32 * q : 32 * (q + 1)]
+                r, b = rs[i // 2][:, c : c + 1], nmr[i // 2][:, c : c + 1]
+                if eng == "A":
+                    nc.scalar.activation(dst, src, ACT.Identity, bias=b, scale=r)
+                else:
+                    e = nc.vector if eng == "V" else nc.gpsimd
+                    e.tensor_scalar(out=dst, in0=src, scalar1=r, scalar2=b, op0=ALU.mult, op1=ALU.add)
+            gh[i, g] = t
+
+        tbank = {}
+
+        def turn_g(h, g, tp):
+            bank = psum.tile([P, 2, 2, P], F32, name="tr", tag="tr", bufs=2)
+            for u in range(2):
+                for l in range(2):
+                    nc.tensor.transpose(bank[:, u, l, :], gh[2 * h + l, g][:, 2 * tp + u, :], ident[:])
+            tbank[h, g, tp] = bank
+
+        def affine(h, g, tp):
+            if tp == 0:
+                gT[h, g] = work.tile([P, PACK, HALF], F32, name="gT", tag="gT", bufs=3)
+            for u in range(2):
+                t = 2 * tp + u
+                nc.scalar.activation(
+                    gT[h, g][:, t, :], tbank[h, g, tp][:, u, :, :].rearrange("p l n -> p (l n)"), ACT.Identity,
+                    bias=b_col[:, g, t : t + 1], scale=w_col[:, g, t : t + 1],
+                )
+
+        def gate_mul(h, g):
+            hb[h, g] = work.tile([P, HALF, PACK], BF16, name="hb", tag="hb", bufs=3, align_bytes=64)
+            nc.vector.tensor_tensor(
+                out=hb[h, g][:].rearrange("p (c i) t -> p c t i", i=4),
+                in0=gT[h, g][:].rearrange("p t (c i) -> p c t i", i=4),
+                in1=sp[g][:, :, HALF * h : HALF * (h + 1)].rearrange("p t (c i) -> p c t i", i=4),
+                op=ALU.mult,
+            )
+
+        def quant_h(h, g):
+            nc.vector.quantize_mx(
+                out=hc[h][g][:].bitcast(FP8X4), scales=hcs[h][g][:], in_=hb[h, g][:].rearrange("p r t -> p (r t)")
+            )
+
+        acc2 = {}
+
+        def out_mx(h, k, g):
+            l, n = divmod(k, 4)
+            if g == 0:
+                acc2[h, k] = psum.tile([P, TOK], F32, name="mx", tag="mx", bufs=SWEEP)
+            nc.tensor.matmul_mx(
+                out=acc2[h, k][:],
+                lhsT=hc[h][g][:, P * l : P * (l + 1)].bitcast(FP8X4),
+                lhsT_scale=hcs[h][g][:, P * l : P * (l + 1)],
+                rhs=wo[g][:, 2 * KP * n : 2 * KP * (n + 1)].bitcast(FP4X4),
+                rhs_scale=wos[:, g, KP * n : KP * (n + 1)],
+                start=(g == 0),
+                stop=(g == NP - 1),
+            )
+
+        o_tile = {}
+
+        def finish(h, k):
+            n = k % 4
+            o = work.tile([P, KP], F32, name="o", tag="o", bufs=6)
+            nc.vector.tensor_tensor(
+                out=o[:], in0=acc2[h, k][:], in1=bo_bc[:, KP * n : KP * (n + 1)], op=ALU.add
+            )
+            o_tile[h, k] = o
+
+        def store(h, k):
+            l, n = divmod(k, 4)
+            i = 2 * h + l
+            nc.sync.dma_start(out=out[0, P * i : P * (i + 1), KP * n : KP * (n + 1)], in_=o_tile[h, k][:])
+
+        def gate_tile(j):
+            for g in range(NP):
+                gate_mx(j, g)
+
+        def out_tile(h, k):
+            for g in range(NP):
+                out_mx(h, k, g)
+
+        nc.sync.dma_start(out=xb0[:], in_=x_tok[:, :, 0:KP])
+        load_x_scale(0)
+        nc.sync.dma_start(out=xb1[:], in_=x_tok[:, :, KP:E])
+        load_x_scale(1)
+        load_attn(0)
+        load_scales(wgs[0], Wg_scales[:, :, first_cols[0]])
+        load_x_scale(2)
+        load_wg(0, 0)
+        load_x_scale(3)
+        load_wg(0, 1)
+        load_attn(1)
+        load_wg(0, 2)
+        load_wg(0, 3)
+        load_wg(1, 0)
+        load_wg(1, 1)
+        load_wg(1, 2)
+        load_wg(1, 3)
+        load_scales(wgs[1], Wg_scales[:, :, first_cols[1]])
+        load_attn(2)
+        load_attn(3)
+        nc.sync.dma_start(out=wo[0][:], in_=Wo_words[0])
+        nc.sync.dma_start(out=wo[1][:], in_=Wo_words[1])
+        nc.sync.dma_start(out=wo[2][:], in_=Wo_words[2])
+        nc.sync.dma_start(out=wo[3][:], in_=Wo_words[3])
+        dequant(0, 0)
+        dequant(0, 1)
+        dequant(0, 2)
+        turn_x(0, 0)
+        dequant(0, 3)
+        lay_x(0, 0)
+        dequant(1, 0)
+        turn_x(0, 1)
+        dequant(1, 1)
+        lay_x(0, 1)
+        dequant(1, 2)
+        turn_x(1, 0)
+        bgp = psum.tile([P, TOK], F32, name="mx", tag="mx", bufs=SWEEP)
+        nc.tensor.transpose(bgp[:, 0:P], bg_sq[:], ident[:])
+        nc.scalar.copy(out=bg_col[:], in_=bgp[:, 0:NJ])
+        sums(0, 0)
+        quant_x(0)
+        dequant(1, 3)
+        lay_x(1, 0)
+        dequant(2, 0)
+        turn_x(1, 1)
+        sums(0, 1)
+        dequant(2, 1)
+        gate_mx(0, 0)
+        gate_mx(1, 0)
+        lay_x(1, 1)
+        dequant(2, 2)
+        gate_mx(2, 0)
+        turn_x(2, 0)
+        sums(0, 2)
+        dequant(2, 3)
+        gate_mx(3, 0)
+        dequant(3, 0)
+        gate_mx(4, 0)
+        gate_mx(5, 0)
+        lay_x(2, 0)
+        dequant(3, 1)
+        turn_x(2, 1)
+        sums(0, 3)
+        quant_x(1)
+        turn_x(3, 0)
+        dequant(3, 2)
+        lay_x(2, 1)
+        mean0()
+        gate_mx(0, 1)
+        gate_mx(1, 1)
+        dequant(3, 3)
+        lay_x(3, 0)
+        gate_mx(2, 1)
+        gate_mx(3, 1)
+        quant_x(2)
+        squares(0, 0)
+        turn_x(3, 1)
+        stats(1, 0)
+        gate_mx(4, 1)
+        gate_mx(5, 1)
+        lay_x(3, 1)
+        gate_mx(0, 2)
+        gate_mx(1, 2)
+        squares(0, 1)
+        quant_x(3)
+        gate_mx(2, 2)
+        gate_mx(3, 2)
+        stats(1, 1)
+        gate_mx(4, 2)
+        squares(0, 2)
+        gate_mx(5, 2)
+        gate_mx(0, 3)
+        stats(1, 2)
+        gate_mx(1, 3)
+        gate_mx(2, 3)
+        silu(0)
+        stats(1, 3)
+        gate_mx(3, 3)
+        gate_mx(4, 3)
+        squares(0, 3)
+        store_s(0)
+        gate_mx(5, 3)
+        load_scales(wos, Wo_scales)
+        gate_tile(6)
+        silu(1)
+        variance(0)
+        silu(2)
+        store_s(1)
+        gate_tile(7)
+        silu(3)
+        store_s(2)
+        seed(0)
+        stats(2, 0)
+        newton(0)
+        silu(4)
+        store_s(3)
+        gate_tile(8)
+        stats(2, 1)
+        silu(6)
+        store_s(4)
+        silu(5)
+        stats(2, 2)
+        store_s(6)
+        gate_tile(9)
+        silu(7)
+        store_s(5)
+        stats(2, 3)
+        silu(8)
+        store_s(7)
+        gate_tile(10)
+        store_s(8)
+        silu(9)
+        norm(0, 2, "V")
+        norm(1, 2, "V")
+        gate_tile(11)
+        norm(0, 0, "A")
+        store_s(9)
+        norm(0, 3, "V")
+        norm(1, 0, "A")
+        norm(1, 3, "V")
+        stats(3, 0)
+        silu(10)
+        turn_g(0, 0, 0)
+        gate_tile(12)
+        stats(3, 1)
+        norm(0, 1, "A")
+        store_s(10)
+        stats(3, 2)
+        affine(0, 0, 0)
+        turn_g(0, 0, 1)
+        stats(3, 3)
+        gate_tile(13)
+        norm(1, 1, "A")
+        variance(1)
+        affine(0, 0, 1)
+        turn_g(0, 1, 0)
+        silu(11)
+        gate_tile(14)
+        seed(1)
+        affine(0, 1, 0)
+        store_s(11)
+        gate_mul(0, 0)
+        newton(1)
+        turn_g(0, 1, 1)
+        silu(12)
+        gate_tile(15)
+        quant_h(0, 0)
+        silu(13)
+        store_s(12)
+        affine(0, 1, 1)
+        store_s(13)
+        out_mx(0, 0, 0)
+        out_mx(0, 1, 0)
+        silu(14)
+        gate_mul(0, 1)
+        turn_g(0, 2, 0)
+        out_mx(0, 2, 0)
+        silu(15)
+        store_s(14)
+        out_mx(0, 3, 0)
+        turn_g(0, 2, 1)
+        affine(0, 2, 0)
+        store_s(15)
+        quant_h(0, 1)
+        out_mx(0, 4, 0)
+        nc.sync.dma_start(out=bo_bc[:], in_=bo.partition_broadcast(P))
+        norm(2, 2, "V")
+        out_mx(0, 5, 0)
+        affine(0, 2, 1)
+        turn_g(0, 3, 0)
+        norm(3, 2, "V")
+        out_mx(0, 0, 1)
+        affine(0, 3, 0)
+        gate_mul(0, 2)
+        turn_g(0, 3, 1)
+        out_mx(0, 1, 1)
+        affine(0, 3, 1)
+        out_mx(0, 2, 1)
+        out_mx(0, 3, 1)
+        quant_h(0, 2)
+        out_mx(0, 4, 1)
+        norm(2, 0, "A")
+        norm(2, 3, "V")
+        out_mx(0, 5, 1)
+        out_mx(0, 0, 2)
+        norm(3, 0, "A")
+        out_mx(0, 1, 2)
+        gate_mul(0, 3)
+        out_mx(0, 2, 2)
+        out_mx(0, 3, 2)
+        norm(2, 1, "A")
+        out_mx(0, 4, 2)
+        turn_g(1, 0, 0)
+        quant_h(0, 3)
+        norm(3, 1, "A")
+        out_mx(0, 5, 2)
+        norm(3, 3, "V")
+        out_mx(0, 0, 3)
+        out_mx(0, 1, 3)
+        affine(1, 0, 0)
+        finish(0, 0)
+        turn_g(1, 0, 1)
+        out_mx(0, 2, 3)
+        finish(0, 1)
+        affine(1, 0, 1)
+        store(0, 0)
+        turn_g(1, 1, 0)
+        out_mx(0, 3, 3)
+        finish(0, 2)
+        store(0, 1)
+        affine(1, 1, 0)
+        out_mx(0, 4, 3)
+        out_mx(0, 5, 3)
+        gate_mul(1, 0)
+        store(0, 2)
+        turn_g(1, 1, 1)
+        turn_g(1, 2, 0)
+        affine(1, 1, 1)
+        out_tile(0, 6)
+        finish(0, 3)
+        affine(1, 2, 0)
+        finish(0, 4)
+        store(0, 3)
+        out_tile(0, 7)
+        quant_h(1, 0)
+        store(0, 4)
+        finish(0, 5)
+        turn_g(1, 2, 1)
+        finish(0, 6)
+        store(0, 5)
+        out_mx(1, 0, 0)
+        affine(1, 2, 1)
+        finish(0, 7)
+        out_mx(1, 1, 0)
+        store(0, 6)
+        turn_g(1, 3, 0)
+        gate_mul(1, 1)
+        store(0, 7)
+        turn_g(1, 3, 1)
+        affine(1, 3, 0)
+        out_mx(1, 2, 0)
+        out_mx(1, 3, 0)
+        affine(1, 3, 1)
+        out_mx(1, 4, 0)
+        quant_h(1, 1)
+        out_mx(1, 5, 0)
+        gate_mul(1, 2)
+        out_mx(1, 0, 1)
+        out_mx(1, 1, 1)
+        out_mx(1, 2, 1)
+        out_mx(1, 3, 1)
+        quant_h(1, 2)
+        out_mx(1, 4, 1)
+        gate_mul(1, 3)
+        out_mx(1, 5, 1)
+        out_mx(1, 0, 2)
+        out_mx(1, 1, 2)
+        out_mx(1, 2, 2)
+        quant_h(1, 3)
+        out_mx(1, 3, 2)
+        out_mx(1, 4, 2)
+        out_mx(1, 5, 2)
+        out_mx(1, 0, 3)
+        out_mx(1, 1, 3)
+        finish(1, 0)
+        out_mx(1, 2, 3)
+        out_mx(1, 3, 3)
+        finish(1, 1)
+        out_mx(1, 4, 3)
+        store(1, 0)
+        out_mx(1, 5, 3)
+        finish(1, 2)
+        out_tile(1, 6)
+        store(1, 1)
+        finish(1, 3)
+        store(1, 2)
+        finish(1, 4)
+        out_tile(1, 7)
+        store(1, 3)
+        finish(1, 5)
+        store(1, 4)
+        store(1, 5)
+        finish(1, 6)
+        finish(1, 7)
+        store(1, 6)
+        store(1, 7)

@@ -16,6 +16,7 @@ ACT = mybir.ActivationFunctionType
 
 P = 128
 TOK = 512
+HALF = TOK // 2
 E = 2048
 PACK = 4
 KP = P * PACK
@@ -27,7 +28,6 @@ EPS = 1e-5
 RSQRT_MAGIC = 1597463007.0
 FLOPS = 2 * 2 * TOK * E * E
 SWEEP = 6
-HALF = TOK // 2
 SPLIT = (P * SWEEP, E - P * SWEEP)
 
 
@@ -47,8 +47,8 @@ def tile_multiscaleretention_pb_w4_kernel(
 
         xb0 = keep.tile([P, NI, KP], U8, name="xb0", align_bytes=64)
         xb1 = keep.tile([P, NI, E - KP], U8, name="xb1", align_bytes=64)
-        xs = [keep.tile([P, KP], F32, name="xs%d" % g) for g in range(NP)]
-        wgs = [keep.tile([P, NP, n], U8, name="wgs%d" % k, align_bytes=64) for k, n in enumerate(SPLIT)]
+        xs = keep.tile([P, NP, PACK], F32, name="xs")
+        wgs = keep.tile([P, NP, E], U8, name="wgs", align_bytes=64)
         wos = keep.tile([P, NP, E], U8, name="wos", align_bytes=64)
         wg = [
             [keep.tile([P, 2 * n], U8, name="wg%d%d" % (k, g), align_bytes=64) for g in range(NP)]
@@ -56,7 +56,9 @@ def tile_multiscaleretention_pb_w4_kernel(
         ]
         wo = [keep.tile([P, 2 * E], U8, name="wo%d" % g, align_bytes=64) for g in range(NP)]
         at = [keep.tile([P, E], BF16, name="at%d" % i) for i in range(NI)]
+        bo_row = keep.tile([P, E], BF16, name="bo_row")
         bo_bc = keep.tile([P, E], BF16, name="bo_bc")
+        ones = keep.tile([P, P], BF16, name="ones")
         bg_rows = keep.tile([NJ, P], BF16, name="bg_rows")
         bg_sq = keep.tile([P, P], F32, name="bg_sq")
         bg_col = keep.tile([P, NJ], F32, name="bg_col")
@@ -72,44 +74,32 @@ def tile_multiscaleretention_pb_w4_kernel(
         hcs = [[keep.tile([P, HALF], U8, name="hcs%d%d" % (h, g), align_bytes=64) for g in range(NP)] for h in range(2)]
         sp = [keep.tile([P, PACK, TOK], F32, name="sp%d" % g) for g in range(NP)]
         NC = 2 * NJ
-        st, var, yi, y0, rs, nmr = ([] for k in range(6))
-        for k in range(2):
-            st.append(keep.tile([P, NC, 6], F32, name="st%d" % k))
-            var.append(keep.tile([P, NC], F32, name="var%d" % k))
-            yi.append(keep.tile([P, NC], I32, name="yi%d" % k))
-            y0.append(keep.tile([P, NC], I32, name="y0%d" % k))
-            rs.append(keep.tile([P, NC], F32, name="rs%d" % k))
-            nmr.append(keep.tile([P, NC], F32, name="nmr%d" % k))
-        ssum = keep.tile([P, NJ], F32, name="ssum")
-        nmean = keep.tile([P, NC], F32, name="nmean")
-        m2 = keep.tile([P, NJ], F32, name="m2")
+        st = [keep.tile([P, NC, 6], F32, name="st%d" % h) for h in range(2)]
+        var = [keep.tile([P, NC], F32, name="var%d" % h) for h in range(2)]
+        half_bits = [keep.tile([P, NC], I32, name="hb%d" % h) for h in range(2)]
+        y0 = [keep.tile([P, NC], I32, name="y0%d" % h) for h in range(2)]
+        rs = [keep.tile([P, NC], F32, name="rs%d" % h) for h in range(2)]
+        nmr = [keep.tile([P, NC], F32, name="nmr%d" % h) for h in range(2)]
 
-        x_scale_row = x_scale.rearrange("o u k -> (o u k)")
-
-        def load_x_scale(g):
-            nc.sync.dma_start(out=xs[g][:], in_=x_scale_row[KP * g : KP * (g + 1)].partition_broadcast(P))
-
-        nc.scalar.dma_start(out=bg_rows[:], in_=bg.rearrange("(j q) -> j q", q=P))
-        nc.scalar.dma_start(out=w_raw[:], in_=gn_w.rearrange("(g p t) -> p g t", p=P, t=PACK))
-        nc.scalar.dma_start(out=b_raw[:], in_=gn_b.rearrange("(g p t) -> p g t", p=P, t=PACK))
+        nc.sync.dma_start(out=xb0[:], in_=x_tok[:, :, 0:KP])
+        nc.scalar.dma_start(out=xs[:], in_=x_scale.rearrange("o u (g p t) -> p (o u g) t", p=P, t=PACK))
+        nc.sync.dma_start(out=xb1[:], in_=x_tok[:, :, KP:E])
 
         nc.vector.memset(warm[:], 0.0)
-        for k in range(2):
-            nc.vector.memset(wgs[k][:].rearrange("p g n -> p (g n)").bitcast(I32), 0)
+        nc.vector.memset(wgs[:].rearrange("p g n -> p (g n)").bitcast(I32), 0)
+        nc.vector.memset(wos[:].rearrange("p g n -> p (g n)").bitcast(I32), 0)
         nc.scalar.activation(warm[:], warm[:], ACT.Silu)
         make_identity(nc, ident[:])
-        nc.gpsimd.memset(wos[:].rearrange("p g n -> p (g n)").bitcast(I32), 0)
+        nc.gpsimd.memset(bo_row[:].bitcast(I32), 0)
+        nc.gpsimd.memset(ones[:], 1.0)
         nc.gpsimd.memset(bg_sq[:], 0.0)
-        nc.gpsimd.tensor_copy(out=bg_sq[0:NJ, :], in_=bg_rows[:])
-        nc.gpsimd.tensor_copy(out=w_col[:], in_=w_raw[:])
-        nc.gpsimd.tensor_copy(out=b_col[:], in_=b_raw[:])
+
+        first_cols = (slice(0, SPLIT[0]), slice(SPLIT[0], E))
 
         def load_scales(plane, scales):
             view = scales.rearrange("g (q r) n -> r q g n", r=4)
             for r in range(4):
                 nc.sync.dma_start(out=plane[r:P:32, :, :].bitcast(I32), in_=view[r].bitcast(I32))
-
-        first_cols = (slice(0, SPLIT[0]), slice(SPLIT[0], E))
 
         def load_wg(k, g):
             lo, hi = first_cols[k].start, first_cols[k].stop
@@ -118,31 +108,49 @@ def tile_multiscaleretention_pb_w4_kernel(
         def load_attn(i):
             nc.sync.dma_start(out=at[i][:], in_=attn_tok[:, i, :])
 
+        def load_small():
+            nc.sync.dma_start(out=bg_rows[:], in_=bg.rearrange("(j q) -> j q", q=P))
+            nc.sync.dma_start(out=bo_row[0:1, :], in_=bo.rearrange("(o n) -> o n", o=1))
+            nc.sync.dma_start(out=w_raw[:], in_=gn_w.rearrange("(g p t) -> p g t", p=P, t=PACK))
+            nc.sync.dma_start(out=b_raw[:], in_=gn_b.rearrange("(g p t) -> p g t", p=P, t=PACK))
+            nc.gpsimd.tensor_copy(out=bg_sq[0:NJ, :], in_=bg_rows[:])
+            nc.gpsimd.tensor_copy(out=w_col[:], in_=w_raw[:])
+            nc.gpsimd.tensor_copy(out=b_col[:], in_=b_raw[:])
 
-        xd = {}
+        def load_wo(g):
+            nc.sync.dma_start(out=wo[g][:], in_=Wo_words[g])
+
+        xw = {}
         xg = {}
         xbank = {}
 
-        def dequant(g, i):
-            t = work.tile([P, KP], BF16, name="xd", tag="xd", bufs=8, align_bytes=64)
+        def widen(g, i, eng):
+            t = work.tile([P, KP], BF16, name="xw", tag="xw", bufs=10, align_bytes=64)
             src = xb0[:, i, :] if g == 0 else xb1[:, i, KP * (g - 1) : KP * g]
-            nc.vector.tensor_tensor(out=t[:], in0=src.bitcast(FP8), in1=xs[g][:], op=ALU.mult)
-            xd[g, i] = t
+            if eng == "V":
+                nc.vector.tensor_copy(out=t[:], in_=src.bitcast(FP8))
+            else:
+                nc.scalar.copy(out=t[:], in_=src.bitcast(FP8))
+            xw[g, i] = t
 
         def turn_x(g, b):
             bank = psum.tile([P, 2, 2, P], F32, name="tr", tag="tr", bufs=2)
             for l in range(2):
-                words = xd[g, 2 * b + l][:].bitcast(F32)
+                words = xw[g, 2 * b + l][:].bitcast(F32)
                 for u in range(2):
                     nc.tensor.transpose(bank[:, u, l, :], words[:, u : KP // 2 : 2], ident[:])
             xbank[g, b] = bank
 
-        def lay_x(g, b):
+        def scale_x(g, b):
             if b == 0:
                 xg[g] = work.tile([P, TOK, PACK], BF16, name="xg", tag="xg", bufs=2, align_bytes=64)
-            half = xg[g][:, 2 * P * b : 2 * P * (b + 1), :]
-            nc.scalar.copy(
-                out=half.bitcast(F32), in_=xbank[g, b][:].rearrange("p u l r -> p (l r) u")
+            half = xg[g][:, HALF * b : HALF * (b + 1), :]
+            scale = xs[:, g, :].rearrange("p (u e) -> p u e", e=2).unsqueeze(1)
+            nc.vector.tensor_tensor(
+                out=half.rearrange("p r (u e) -> p r u e", e=2),
+                in0=xbank[g, b][:].bitcast(BF16).rearrange("p u l (r e) -> p (l r) u e", e=2),
+                in1=scale.to_broadcast([P, HALF, 2, 2]),
+                op=ALU.mult,
             )
 
         def quant_x(g):
@@ -160,7 +168,7 @@ def tile_multiscaleretention_pb_w4_kernel(
             nc.tensor.matmul_mx(
                 out=acc[j][:],
                 lhsT=wg[k][g][:, 2 * P * c : 2 * P * (c + 1)].bitcast(FP4X4),
-                lhsT_scale=wgs[k][:, g, P * c : P * (c + 1)],
+                lhsT_scale=wgs[:, g, P * j : P * (j + 1)],
                 rhs=xc[g][:].bitcast(FP8X4),
                 rhs_scale=xcs[g][:],
                 start=(g == 0),
@@ -172,13 +180,12 @@ def tile_multiscaleretention_pb_w4_kernel(
             nc.scalar.activation(s[:], acc[j][:], ACT.Silu, bias=bg_col[:, j : j + 1])
             s_tile[j] = s
 
-        def store_s(j):
-            g, q = divmod(j, 4)
-            for t in range(PACK):
-                nc.sync.dma_start(out=sp[g][32 * q : 32 * (q + 1), t, :], in_=s_tile[j][t:P:4, :])
+        def spread(j):
+            nc.sync.dma_start(out=scratch[P * j : P * (j + 1), :], in_=s_tile[j][:])
 
-        def load_s(g):
-            pass
+        def fetch(g):
+            rows = scratch[KP * g : KP * (g + 1), :]
+            nc.sync.dma_start(out=sp[g][:], in_=rows.rearrange("(p t) n -> p t n", t=PACK))
 
         gh = {}
         gT = {}
@@ -188,87 +195,80 @@ def tile_multiscaleretention_pb_w4_kernel(
             return slice(KP * g + GRP * q, KP * g + GRP * (q + 1))
 
         def stats(i, g):
-            for q in range(4):
+            def one(q):
                 c = NJ * (i % 2) + 4 * g + q
-                nc.vector.bn_stats(out=st[i // 2][:, c, :], in_=at[i][:, channels(g, q)])
+                return lambda: nc.vector.bn_stats(out=st[i // 2][:, c, :], in_=at[i][:, channels(g, q)])
+            return [one(q) for q in range(4)]
 
-        def sums(i, g):
-            for q in range(4):
-                c = 4 * g + q
-                junk = work.tile([P, GRP], BF16, name="junk", tag="junk", bufs=2)
-                nc.scalar.activation(junk[:], at[0][:, channels(g, q)], ACT.Identity, accum_out=ssum[:, c : c + 1])
+        def small(name):
+            return work.tile([P, NC], F32, name=name, tag=name, bufs=2)
 
-        def squares(i, g):
-            for q in range(4):
-                c = 4 * g + q
-                junk = work.tile([P, GRP], BF16, name="junk", tag="junk", bufs=2)
-                nc.scalar.activation(
-                    junk[:], at[0][:, channels(g, q)], ACT.Square,
-                    bias=nmean[:, c : c + 1], accum_out=m2[:, c : c + 1],
-                )
+        def rsqrt_steps(h):
+            me, m2e, mo, m2o = (st[h][:, :, f] for f in (1, 2, 4, 5))
+            V = nc.vector
+            d, v, q, sm = small("d"), small("v"), small("q"), small("sm")
+            steps = [
+                lambda: V.tensor_tensor(out=d[:], in0=me, in1=mo, op=ALU.subtract),
+                lambda: V.scalar_tensor_tensor(out=v[:], in0=m2e, scalar=GRP * EPS, in1=m2o, op0=ALU.add, op1=ALU.add),
+                lambda: V.scalar_tensor_tensor(out=q[:], in0=d[:], scalar=0.25, in1=d[:], op0=ALU.mult, op1=ALU.mult),
+                lambda: V.tensor_tensor(out=sm[:], in0=me, in1=mo, op=ALU.add),
+                lambda: V.scalar_tensor_tensor(
+                    out=var[h][:], in0=v[:], scalar=1.0 / GRP, in1=q[:], op0=ALU.mult, op1=ALU.add
+                ),
+                lambda: V.tensor_scalar(
+                    out=half_bits[h][:], in0=var[h][:].bitcast(I32), scalar1=1, scalar2=None, op0=ALU.arith_shift_right
+                ),
+                lambda: V.tensor_scalar(
+                    out=y0[h][:], in0=half_bits[h][:], scalar1=-1.0, scalar2=RSQRT_MAGIC, op0=ALU.mult, op1=ALU.add
+                ),
+            ]
 
-        def mean0():
-            nc.gpsimd.tensor_scalar(
-                out=nmean[:, 0:NJ], in0=ssum[:], scalar1=-1.0 / GRP, scalar2=0.0, op0=ALU.mult, op1=ALU.add
-            )
-
-        def small(name, n=2 * NJ):
-            return work.tile([P, n], F32, name=name, tag=name + str(n), bufs=2)
-
-        def variance(k):
-            lo = 0
-            if k == 0:
-                lo = NJ
-                nc.gpsimd.tensor_scalar(
-                    out=var[0][:, 0:NJ], in0=m2[:], scalar1=1.0 / GRP, scalar2=EPS, op0=ALU.mult, op1=ALU.add
-                )
-            n = NC - lo
-            me, m2e, mo, m2o = (st[k][:, lo:NC, f] for f in (1, 2, 4, 5))
-            d, dd, v, q = small("d", n), small("dd", n), small("v", n), small("q", n)
-            nc.gpsimd.tensor_tensor(out=d[:], in0=me, in1=mo, op=ALU.subtract)
-            nc.gpsimd.tensor_tensor(out=v[:], in0=m2e, in1=m2o, op=ALU.add)
-            nc.gpsimd.tensor_tensor(out=dd[:], in0=d[:], in1=d[:], op=ALU.mult)
-            nc.gpsimd.tensor_scalar(out=v[:], in0=v[:], scalar1=1.0 / GRP, scalar2=EPS, op0=ALU.mult, op1=ALU.add)
-            nc.gpsimd.tensor_scalar(out=q[:], in0=dd[:], scalar1=0.25, scalar2=0.0, op0=ALU.mult, op1=ALU.add)
-            nc.gpsimd.tensor_tensor(out=var[k][:, lo:NC], in0=v[:], in1=q[:], op=ALU.add)
-
-        def seed(k):
-            nc.vector.tensor_scalar(
-                out=yi[k][:], in0=var[k][:].bitcast(I32), scalar1=1, scalar2=None, op0=ALU.arith_shift_right
-            )
-            nc.vector.tensor_scalar(
-                out=y0[k][:], in0=yi[k][:], scalar1=-1.0, scalar2=RSQRT_MAGIC, op0=ALU.mult, op1=ALU.add
-            )
-
-        def newton(k):
-            y = y0[k][:].bitcast(F32)
-            for step in range(3):
+            def round(y, last):
                 a, b = small("na"), small("nb")
-                last = rs[k] if step == 2 else small("ny")
-                nc.gpsimd.tensor_tensor(out=a[:], in0=y, in1=y, op=ALU.mult)
-                nc.gpsimd.tensor_tensor(out=b[:], in0=a[:], in1=var[k][:], op=ALU.mult)
-                nc.gpsimd.tensor_scalar(out=b[:], in0=b[:], scalar1=-0.5, scalar2=1.5, op0=ALU.mult, op1=ALU.add)
-                nc.gpsimd.tensor_tensor(out=last[:], in0=y, in1=b[:], op=ALU.mult)
-                y = last[:]
-            lo = NJ if k == 0 else 0
-            nm = nmean if k == 0 else small("nm")
-            nc.gpsimd.tensor_tensor(out=nm[:, lo:NC], in0=st[k][:, lo:NC, 1], in1=st[k][:, lo:NC, 4], op=ALU.add)
-            nc.gpsimd.tensor_scalar(out=nm[:, lo:NC], in0=nm[:, lo:NC], scalar1=-0.5, scalar2=0.0, op0=ALU.mult, op1=ALU.add)
-            nc.gpsimd.tensor_tensor(out=nmr[k][:], in0=nm[:], in1=rs[k][:], op=ALU.mult)
+                return [
+                    lambda: V.tensor_tensor(out=a[:], in0=y, in1=y, op=ALU.mult),
+                    lambda: V.scalar_tensor_tensor(
+                        out=b[:], in0=a[:], scalar=-0.5, in1=var[h][:], op0=ALU.mult, op1=ALU.mult
+                    ),
+                    lambda: V.scalar_tensor_tensor(out=last, in0=b[:], scalar=1.5, in1=y, op0=ALU.add, op1=ALU.mult),
+                ]
+
+            y1, y2 = small("y1"), small("y2")
+            steps += round(y0[h][:].bitcast(F32), y1[:]) + round(y1[:], y2[:]) + round(y2[:], rs[h][:])
+            steps.append(
+                lambda: V.scalar_tensor_tensor(
+                    out=nmr[h][:], in0=sm[:], scalar=-0.5, in1=rs[h][:], op0=ALU.mult, op1=ALU.mult
+                )
+            )
+            return steps
+
+        def weave(main, side):
+            for k, one in enumerate(main):
+                one()
+                if k < len(side):
+                    side[k]()
+            for one in side[len(main) :]:
+                one()
 
         def norm(i, g, eng):
             t = work.tile([P, PACK, P], F32, name="gh", tag="gh", bufs=10)
-            for q in range(4):
+            gh[i, g] = t
+
+            def one(q):
                 c = NJ * (i % 2) + 4 * g + q
                 src = at[i][:, channels(g, q)].rearrange("p (m t) -> p t m", t=PACK)
                 dst = t[:, :, 32 * q : 32 * (q + 1)]
                 r, b = rs[i // 2][:, c : c + 1], nmr[i // 2][:, c : c + 1]
                 if eng == "A":
-                    nc.scalar.activation(dst, src, ACT.Identity, bias=b, scale=r)
-                else:
-                    e = nc.vector if eng == "V" else nc.gpsimd
-                    e.tensor_scalar(out=dst, in0=src, scalar1=r, scalar2=b, op0=ALU.mult, op1=ALU.add)
-            gh[i, g] = t
+                    return lambda: nc.scalar.activation(dst, src, ACT.Identity, bias=b, scale=r)
+                return lambda: nc.vector.tensor_scalar(
+                    out=dst, in0=src, scalar1=r, scalar2=b, op0=ALU.mult, op1=ALU.add
+                )
+            return [one(q) for q in range(4)]
+
+        def norm_pair(h, g):
+            for l in range(2):
+                weave(norm(2 * h + l, g, "A"), [])
 
         tbank = {}
 
@@ -319,6 +319,24 @@ def tile_multiscaleretention_pb_w4_kernel(
                 stop=(g == NP - 1),
             )
 
+        bo_bank = {}
+
+        def bo_mm(n):
+            bo_bank[n] = psum.tile([P, KP], F32, name="mx", tag="mx", bufs=SWEEP)
+            nc.tensor.matmul(bo_bank[n][:], lhsT=ones[:], rhs=bo_row[:, KP * n : KP * (n + 1)], start=True, stop=True)
+
+        def bo_copy(n):
+            nc.scalar.copy(out=bo_bc[:, KP * n : KP * (n + 1)], in_=bo_bank[n][:])
+
+        bg_bank = {}
+
+        def bg_turn():
+            bg_bank[0] = psum.tile([P, TOK], F32, name="tr", tag="tr", bufs=2)
+            nc.tensor.transpose(bg_bank[0][:, 0:P], bg_sq[:], ident[:])
+
+        def bg_copy():
+            nc.scalar.copy(out=bg_col[:], in_=bg_bank[0][:, 0:NJ])
+
         o_tile = {}
 
         def finish(h, k):
@@ -334,288 +352,286 @@ def tile_multiscaleretention_pb_w4_kernel(
             i = 2 * h + l
             nc.sync.dma_start(out=out[0, P * i : P * (i + 1), KP * n : KP * (n + 1)], in_=o_tile[h, k][:])
 
-        def gate_tile(j):
-            for g in range(NP):
-                gate_mx(j, g)
+        def gate_tiles(*js):
+            for j in js:
+                for g in range(NP):
+                    gate_mx(j, g)
 
         def out_tile(h, k):
             for g in range(NP):
                 out_mx(h, k, g)
 
-        nc.sync.dma_start(out=xb0[:], in_=x_tok[:, :, 0:KP])
-        load_x_scale(0)
-        nc.sync.dma_start(out=xb1[:], in_=x_tok[:, :, KP:E])
-        load_x_scale(1)
-        load_attn(0)
-        load_scales(wgs[0], Wg_scales[:, :, first_cols[0]])
-        load_x_scale(2)
+        def emit(ops):
+            weave(ops, [])
+
+        steps = [rsqrt_steps(0), rsqrt_steps(1)]
+        load_scales(wgs, Wg_scales)
         load_wg(0, 0)
-        load_x_scale(3)
+        load_small()
+        load_attn(0)
         load_wg(0, 1)
-        load_attn(1)
         load_wg(0, 2)
-        load_wg(0, 3)
-        load_wg(1, 0)
-        load_wg(1, 1)
-        load_wg(1, 2)
-        load_wg(1, 3)
-        load_scales(wgs[1], Wg_scales[:, :, first_cols[1]])
-        load_attn(2)
-        load_attn(3)
-        nc.sync.dma_start(out=wo[0][:], in_=Wo_words[0])
-        nc.sync.dma_start(out=wo[1][:], in_=Wo_words[1])
-        nc.sync.dma_start(out=wo[2][:], in_=Wo_words[2])
-        nc.sync.dma_start(out=wo[3][:], in_=Wo_words[3])
-        dequant(0, 0)
-        dequant(0, 1)
-        dequant(0, 2)
+        load_attn(1)
+        widen(0, 0, "V")
+        widen(0, 2, "A")
+        widen(0, 1, "V")
+        widen(0, 3, "A")
         turn_x(0, 0)
-        dequant(0, 3)
-        lay_x(0, 0)
-        dequant(1, 0)
         turn_x(0, 1)
-        dequant(1, 1)
-        lay_x(0, 1)
-        dequant(1, 2)
+        scale_x(0, 0)
+        load_wg(0, 3)
+        widen(1, 0, "A")
+        widen(1, 1, "A")
+        scale_x(0, 1)
+        widen(1, 2, "A")
         turn_x(1, 0)
-        bgp = psum.tile([P, TOK], F32, name="mx", tag="mx", bufs=SWEEP)
-        nc.tensor.transpose(bgp[:, 0:P], bg_sq[:], ident[:])
-        nc.scalar.copy(out=bg_col[:], in_=bgp[:, 0:NJ])
-        sums(0, 0)
-        quant_x(0)
-        dequant(1, 3)
-        lay_x(1, 0)
-        dequant(2, 0)
+        widen(1, 3, "A")
+        load_wg(1, 0)
+        scale_x(1, 0)
+        widen(2, 0, "A")
+        load_wg(1, 1)
         turn_x(1, 1)
-        sums(0, 1)
-        dequant(2, 1)
-        gate_mx(0, 0)
-        gate_mx(1, 0)
-        lay_x(1, 1)
-        dequant(2, 2)
-        gate_mx(2, 0)
+        load_wg(1, 2)
+        widen(2, 1, "A")
+        quant_x(0)
+        widen(2, 2, "A")
         turn_x(2, 0)
-        sums(0, 2)
-        dequant(2, 3)
+        load_wg(1, 3)
+        scale_x(1, 1)
+        load_attn(2)
+        widen(2, 3, "A")
+        gate_mx(0, 0)
+        load_attn(3)
+        gate_mx(1, 0)
+        widen(3, 0, "A")
+        scale_x(2, 0)
+        gate_mx(2, 0)
         gate_mx(3, 0)
-        dequant(3, 0)
+        widen(3, 1, "A")
+        turn_x(2, 1)
+        load_scales(wos, Wo_scales)
+        widen(3, 2, "A")
+        quant_x(1)
+        load_wo(0)
+        turn_x(3, 0)
+        widen(3, 3, "A")
+        scale_x(2, 1)
+        load_wo(1)
         gate_mx(4, 0)
         gate_mx(5, 0)
-        lay_x(2, 0)
-        dequant(3, 1)
-        turn_x(2, 1)
-        sums(0, 3)
-        quant_x(1)
-        turn_x(3, 0)
-        dequant(3, 2)
-        lay_x(2, 1)
-        mean0()
         gate_mx(0, 1)
         gate_mx(1, 1)
-        dequant(3, 3)
-        lay_x(3, 0)
+        scale_x(3, 0)
         gate_mx(2, 1)
-        gate_mx(3, 1)
-        quant_x(2)
-        squares(0, 0)
         turn_x(3, 1)
-        stats(1, 0)
+        quant_x(2)
+        bg_turn()
+        gate_mx(3, 1)
+        bg_copy()
+        scale_x(3, 1)
         gate_mx(4, 1)
         gate_mx(5, 1)
-        lay_x(3, 1)
         gate_mx(0, 2)
         gate_mx(1, 2)
-        squares(0, 1)
-        quant_x(3)
         gate_mx(2, 2)
+        quant_x(3)
         gate_mx(3, 2)
-        stats(1, 1)
         gate_mx(4, 2)
-        squares(0, 2)
+        emit(stats(0, 0))
         gate_mx(5, 2)
         gate_mx(0, 3)
-        stats(1, 2)
         gate_mx(1, 3)
-        gate_mx(2, 3)
+        emit(stats(0, 1))
         silu(0)
-        stats(1, 3)
+        gate_mx(2, 3)
         gate_mx(3, 3)
-        gate_mx(4, 3)
-        squares(0, 3)
-        store_s(0)
-        gate_mx(5, 3)
-        load_scales(wos, Wo_scales)
-        gate_tile(6)
+        emit(stats(0, 2))
         silu(1)
-        variance(0)
+        gate_mx(4, 3)
+        spread(0)
+        gate_mx(5, 3)
         silu(2)
-        store_s(1)
-        gate_tile(7)
+        gate_tiles(6)
+        emit(stats(0, 3))
+        spread(1)
         silu(3)
-        store_s(2)
-        seed(0)
-        stats(2, 0)
-        newton(0)
+        spread(2)
+        emit(stats(1, 0))
         silu(4)
-        store_s(3)
-        gate_tile(8)
-        stats(2, 1)
+        bo_mm(0)
+        spread(3)
+        emit(stats(1, 1))
+        bo_mm(1)
         silu(6)
-        store_s(4)
+        spread(4)
+        gate_tiles(7)
+        emit(stats(1, 2))
         silu(5)
-        stats(2, 2)
-        store_s(6)
-        gate_tile(9)
+        spread(6)
+        emit(stats(1, 3))
+        bo_copy(0)
+        spread(5)
+        load_wo(2)
+        gate_tiles(8)
         silu(7)
-        store_s(5)
-        stats(2, 3)
+        weave(stats(2, 0), steps[0][0:5])
+        spread(7)
+        bo_mm(2)
         silu(8)
-        store_s(7)
-        gate_tile(10)
-        store_s(8)
+        gate_tiles(9)
+        weave(stats(2, 1), steps[0][5:9])
+        bo_copy(1)
+        spread(8)
+        fetch(0)
+        bo_copy(2)
+        gate_tiles(10)
+        weave(stats(2, 2), steps[0][9:13])
         silu(9)
-        norm(0, 2, "V")
-        norm(1, 2, "V")
-        gate_tile(11)
-        norm(0, 0, "A")
-        store_s(9)
-        norm(0, 3, "V")
-        norm(1, 0, "A")
-        norm(1, 3, "V")
-        stats(3, 0)
+        weave(stats(2, 3), steps[0][13:17])
+        spread(9)
+        gate_tiles(11)
         silu(10)
-        turn_g(0, 0, 0)
-        gate_tile(12)
-        stats(3, 1)
-        norm(0, 1, "A")
-        store_s(10)
-        stats(3, 2)
-        affine(0, 0, 0)
-        turn_g(0, 0, 1)
-        stats(3, 3)
-        gate_tile(13)
-        norm(1, 1, "A")
-        variance(1)
-        affine(0, 0, 1)
-        turn_g(0, 1, 0)
+        emit(stats(3, 0))
+        spread(10)
+        emit(norm(0, 0, "A"))
+        gate_tiles(12)
+        emit(stats(3, 1))
         silu(11)
-        gate_tile(14)
-        seed(1)
-        affine(0, 1, 0)
-        store_s(11)
-        gate_mul(0, 0)
-        newton(1)
-        turn_g(0, 1, 1)
+        emit(stats(3, 2))
+        gate_tiles(13)
+        emit(norm(1, 0, "A"))
+        spread(11)
+        fetch(1)
+        emit(stats(3, 3))
         silu(12)
-        gate_tile(15)
-        quant_h(0, 0)
+        turn_g(0, 0, 0)
+        emit(norm(0, 1, "A"))
+        spread(12)
+        weave(norm(0, 2, "V"), steps[1][0:5])
+        gate_tiles(14)
+        affine(0, 0, 0)
+        weave(norm(1, 2, "V"), steps[1][5:9])
         silu(13)
-        store_s(12)
-        affine(0, 1, 1)
-        store_s(13)
-        out_mx(0, 0, 0)
-        out_mx(0, 1, 0)
+        gate_tiles(15)
+        weave(norm(0, 3, "V"), steps[1][9:13])
         silu(14)
-        gate_mul(0, 1)
-        turn_g(0, 2, 0)
-        out_mx(0, 2, 0)
+        spread(13)
+        weave(norm(1, 3, "V"), steps[1][13:17])
+        emit(norm(1, 1, "A"))
+        spread(14)
+        turn_g(0, 0, 1)
+        bo_mm(3)
         silu(15)
-        store_s(14)
-        out_mx(0, 3, 0)
-        turn_g(0, 2, 1)
+        turn_g(0, 1, 0)
+        affine(0, 0, 1)
+        spread(15)
+        fetch(2)
+        load_wo(3)
+        affine(0, 1, 0)
+        gate_mul(0, 0)
+        turn_g(0, 1, 1)
+        affine(0, 1, 1)
+        turn_g(0, 2, 0)
         affine(0, 2, 0)
-        store_s(15)
-        quant_h(0, 1)
-        out_mx(0, 4, 0)
-        nc.sync.dma_start(out=bo_bc[:], in_=bo.partition_broadcast(P))
-        norm(2, 2, "V")
-        out_mx(0, 5, 0)
+        turn_g(0, 2, 1)
+        quant_h(0, 0)
+        gate_mul(0, 1)
         affine(0, 2, 1)
         turn_g(0, 3, 0)
-        norm(3, 2, "V")
-        out_mx(0, 0, 1)
+        fetch(3)
+        out_mx(0, 0, 0)
+        bo_copy(3)
+        out_mx(0, 1, 0)
+        out_mx(0, 2, 0)
         affine(0, 3, 0)
-        gate_mul(0, 2)
+        quant_h(0, 1)
+        out_mx(0, 3, 0)
+        out_mx(0, 4, 0)
+        emit(norm(2, 0, "A"))
+        out_mx(0, 5, 0)
+        out_mx(0, 0, 1)
+        emit(norm(3, 0, "A"))
         turn_g(0, 3, 1)
-        out_mx(0, 1, 1)
+        gate_mul(0, 2)
         affine(0, 3, 1)
+        turn_g(1, 0, 0)
+        affine(1, 0, 0)
+        turn_g(1, 0, 1)
+        quant_h(0, 2)
+        out_mx(0, 1, 1)
+        affine(1, 0, 1)
         out_mx(0, 2, 1)
         out_mx(0, 3, 1)
-        quant_h(0, 2)
+        emit(norm(2, 1, "A"))
         out_mx(0, 4, 1)
-        norm(2, 0, "A")
-        norm(2, 3, "V")
+        gate_mul(1, 0)
         out_mx(0, 5, 1)
         out_mx(0, 0, 2)
-        norm(3, 0, "A")
+        emit(norm(3, 1, "A"))
         out_mx(0, 1, 2)
-        gate_mul(0, 3)
         out_mx(0, 2, 2)
+        gate_mul(0, 3)
+        emit(norm(2, 2, "A"))
         out_mx(0, 3, 2)
-        norm(2, 1, "A")
-        out_mx(0, 4, 2)
-        turn_g(1, 0, 0)
-        quant_h(0, 3)
-        norm(3, 1, "A")
-        out_mx(0, 5, 2)
-        norm(3, 3, "V")
-        out_mx(0, 0, 3)
-        out_mx(0, 1, 3)
-        affine(1, 0, 0)
-        finish(0, 0)
-        turn_g(1, 0, 1)
-        out_mx(0, 2, 3)
-        finish(0, 1)
-        affine(1, 0, 1)
-        store(0, 0)
         turn_g(1, 1, 0)
-        out_mx(0, 3, 3)
-        finish(0, 2)
-        store(0, 1)
-        affine(1, 1, 0)
-        out_mx(0, 4, 3)
-        out_mx(0, 5, 3)
-        gate_mul(1, 0)
-        store(0, 2)
+        emit(norm(3, 2, "A"))
         turn_g(1, 1, 1)
-        turn_g(1, 2, 0)
+        quant_h(1, 0)
+        out_mx(0, 4, 2)
+        quant_h(0, 3)
+        affine(1, 1, 0)
+        out_mx(0, 5, 2)
+        out_mx(0, 0, 3)
         affine(1, 1, 1)
-        out_tile(0, 6)
+        out_mx(0, 1, 3)
+        finish(0, 0)
+        out_mx(0, 2, 3)
+        out_mx(0, 3, 3)
+        emit(norm(2, 3, "A"))
+        finish(0, 1)
+        out_mx(0, 4, 3)
+        store(0, 0)
+        turn_g(1, 2, 0)
+        finish(0, 2)
+        emit(norm(3, 3, "A"))
+        store(0, 1)
+        turn_g(1, 2, 1)
         finish(0, 3)
+        store(0, 2)
+        out_mx(0, 5, 3)
         affine(1, 2, 0)
+        out_tile(0, 6)
         finish(0, 4)
         store(0, 3)
-        out_tile(0, 7)
-        quant_h(1, 0)
-        store(0, 4)
-        finish(0, 5)
-        turn_g(1, 2, 1)
-        finish(0, 6)
-        store(0, 5)
-        out_mx(1, 0, 0)
         affine(1, 2, 1)
-        finish(0, 7)
-        out_mx(1, 1, 0)
-        store(0, 6)
-        turn_g(1, 3, 0)
         gate_mul(1, 1)
-        store(0, 7)
+        store(0, 4)
+        turn_g(1, 3, 0)
         turn_g(1, 3, 1)
         affine(1, 3, 0)
-        out_mx(1, 2, 0)
-        out_mx(1, 3, 0)
+        finish(0, 5)
+        out_tile(0, 7)
         affine(1, 3, 1)
-        out_mx(1, 4, 0)
         quant_h(1, 1)
-        out_mx(1, 5, 0)
+        store(0, 5)
+        finish(0, 6)
+        out_mx(1, 0, 0)
+        finish(0, 7)
+        store(0, 6)
+        out_mx(1, 1, 0)
+        out_mx(1, 2, 0)
         gate_mul(1, 2)
+        out_mx(1, 3, 0)
+        store(0, 7)
+        out_mx(1, 4, 0)
+        out_mx(1, 5, 0)
         out_mx(1, 0, 1)
         out_mx(1, 1, 1)
+        quant_h(1, 2)
         out_mx(1, 2, 1)
         out_mx(1, 3, 1)
-        quant_h(1, 2)
-        out_mx(1, 4, 1)
         gate_mul(1, 3)
+        out_mx(1, 4, 1)
         out_mx(1, 5, 1)
         out_mx(1, 0, 2)
         out_mx(1, 1, 2)

from contextlib import ExitStack

import concourse.mybir as mybir
from concourse.masks import make_identity

F32 = mybir.dt.float32
BF16 = mybir.dt.bfloat16
I32 = mybir.dt.int32
U32 = mybir.dt.uint32
U8 = mybir.dt.uint8
FP8 = mybir.dt.float8_e4m3fn
FP8X4 = mybir.dt.float8_e4m3fn_x4
FP4X4 = mybir.dt.float4_e2m1fn_x4
ALU = mybir.AluOpType
ACT = mybir.ActivationFunctionType

P = 128
TOK = 512
HALF = TOK // 2
E = 2048
PACK = 4
KP = P * PACK
NP = E // KP
NI = TOK // P
NJ = E // P
GRP = 128
EPS = 1e-5
RSQRT_MAGIC = 1597463007.0
FLOPS = 2 * 2 * TOK * E * E
SWEEP = 6
SPLIT = (P * SWEEP, E - P * SWEEP)


def tile_multiscaleretention_pb_w4_kernel(
    tc, x_bytes, x_scale, attn, Wg_words, Wg_scales, bg, gn_w, gn_b, Wo_words, Wo_scales, bo, out
):
    nc = tc.nc
    with ExitStack() as ctx:
        keep = ctx.enter_context(tc.tile_pool(name="keep", bufs=1))
        work = ctx.enter_context(tc.tile_pool(name="work", bufs=2))
        psum = ctx.enter_context(tc.psum_pool(name="psum", bufs=1))
        ctx.enter_context(tc.manual_schedule())

        x_tok = x_bytes.rearrange("o (i p) k -> p (o i) k", p=P)
        attn_tok = attn.rearrange("o (i p) c -> p (o i) c", p=P)
        scratch = out.rearrange("o a b -> (o a b)").rearrange("(c n) -> c n", n=TOK)

        xb0 = keep.tile([P, NI, KP], U8, name="xb0", align_bytes=64)
        xb1 = keep.tile([P, NI, E - KP], U8, name="xb1", align_bytes=64)
        xs = keep.tile([P, NP, PACK], F32, name="xs")
        wgs = keep.tile([P, NP, E], U8, name="wgs", align_bytes=64)
        wos = keep.tile([P, NP, E], U8, name="wos", align_bytes=64)
        wg = [
            [keep.tile([P, 2 * n], U8, name="wg%d%d" % (k, g), align_bytes=64) for g in range(NP)]
            for k, n in enumerate(SPLIT)
        ]
        wo = [keep.tile([P, 2 * E], U8, name="wo%d" % g, align_bytes=64) for g in range(NP)]
        at = [keep.tile([P, E], BF16, name="at%d" % i) for i in range(NI)]
        bo_row = keep.tile([P, E], BF16, name="bo_row")
        bo_bc = keep.tile([P, E], BF16, name="bo_bc")
        ones = keep.tile([P, P], BF16, name="ones")
        bg_rows = keep.tile([NJ, P], BF16, name="bg_rows")
        bg_sq = keep.tile([P, P], F32, name="bg_sq")
        bg_col = keep.tile([P, NJ], F32, name="bg_col")
        w_raw = keep.tile([P, NP, PACK], BF16, name="w_raw")
        b_raw = keep.tile([P, NP, PACK], BF16, name="b_raw")
        w_col = keep.tile([P, NP, PACK], F32, name="w_col")
        b_col = keep.tile([P, NP, PACK], F32, name="b_col")
        ident = keep.tile([P, P], F32, name="ident")
        warm = keep.tile([P, 1], F32, name="warm")
        xc = [keep.tile([P, TOK], U32, name="xc%d" % g, align_bytes=64) for g in range(NP)]
        xcs = [keep.tile([P, TOK], U8, name="xcs%d" % g, align_bytes=64) for g in range(NP)]
        hc = [[keep.tile([P, HALF], U32, name="hc%d%d" % (h, g), align_bytes=64) for g in range(NP)] for h in range(2)]
        hcs = [[keep.tile([P, HALF], U8, name="hcs%d%d" % (h, g), align_bytes=64) for g in range(NP)] for h in range(2)]
        sp = [keep.tile([P, PACK, TOK], F32, name="sp%d" % g) for g in range(NP)]
        NC = 2 * NJ
        st = [keep.tile([P, NC, 6], F32, name="st%d" % h) for h in range(2)]
        var = [keep.tile([P, NC], F32, name="var%d" % h) for h in range(2)]
        half_bits = [keep.tile([P, NC], I32, name="hb%d" % h) for h in range(2)]
        y0 = [keep.tile([P, NC], I32, name="y0%d" % h) for h in range(2)]
        rs = [keep.tile([P, NC], F32, name="rs%d" % h) for h in range(2)]
        nmr = [keep.tile([P, NC], F32, name="nmr%d" % h) for h in range(2)]

        nc.sync.dma_start(out=xb0[:], in_=x_tok[:, :, 0:KP])
        nc.scalar.dma_start(out=xs[:], in_=x_scale.rearrange("o u (g p t) -> p (o u g) t", p=P, t=PACK))
        nc.sync.dma_start(out=xb1[:], in_=x_tok[:, :, KP:E])

        nc.vector.memset(warm[:], 0.0)
        nc.vector.memset(wgs[:].rearrange("p g n -> p (g n)").bitcast(I32), 0)
        nc.vector.memset(wos[:].rearrange("p g n -> p (g n)").bitcast(I32), 0)
        nc.scalar.activation(warm[:], warm[:], ACT.Silu)
        make_identity(nc, ident[:])
        nc.gpsimd.memset(bo_row[:].bitcast(I32), 0)
        nc.gpsimd.memset(ones[:], 1.0)
        nc.gpsimd.memset(bg_sq[:], 0.0)

        first_cols = (slice(0, SPLIT[0]), slice(SPLIT[0], E))

        def load_scales(plane, scales):
            view = scales.rearrange("g (q r) n -> r q g n", r=4)
            for r in range(4):
                nc.sync.dma_start(out=plane[r:P:32, :, :].bitcast(I32), in_=view[r].bitcast(I32))

        def load_wg(k, g):
            lo, hi = first_cols[k].start, first_cols[k].stop
            nc.sync.dma_start(out=wg[k][g][:], in_=Wg_words[g][:, 2 * lo : 2 * hi])

        def load_attn(i):
            nc.sync.dma_start(out=at[i][:], in_=attn_tok[:, i, :])

        def load_small():
            nc.sync.dma_start(out=bg_rows[:], in_=bg.rearrange("(j q) -> j q", q=P))
            nc.sync.dma_start(out=bo_row[0:1, :], in_=bo.rearrange("(o n) -> o n", o=1))
            nc.sync.dma_start(out=w_raw[:], in_=gn_w.rearrange("(g p t) -> p g t", p=P, t=PACK))
            nc.sync.dma_start(out=b_raw[:], in_=gn_b.rearrange("(g p t) -> p g t", p=P, t=PACK))
            nc.gpsimd.tensor_copy(out=bg_sq[0:NJ, :], in_=bg_rows[:])
            nc.gpsimd.tensor_copy(out=w_col[:], in_=w_raw[:])
            nc.gpsimd.tensor_copy(out=b_col[:], in_=b_raw[:])

        def load_wo(g):
            nc.sync.dma_start(out=wo[g][:], in_=Wo_words[g])

        xw = {}
        xg = {}
        xbank = {}

        def widen(g, i, eng):
            t = work.tile([P, KP], BF16, name="xw", tag="xw", bufs=10, align_bytes=64)
            src = xb0[:, i, :] if g == 0 else xb1[:, i, KP * (g - 1) : KP * g]
            if eng == "V":
                nc.vector.tensor_copy(out=t[:], in_=src.bitcast(FP8))
            else:
                nc.scalar.copy(out=t[:], in_=src.bitcast(FP8))
            xw[g, i] = t

        def turn_x(g, b):
            bank = psum.tile([P, 2, 2, P], F32, name="tr", tag="tr", bufs=2)
            for l in range(2):
                words = xw[g, 2 * b + l][:].bitcast(F32)
                for u in range(2):
                    nc.tensor.transpose(bank[:, u, l, :], words[:, u : KP // 2 : 2], ident[:])
            xbank[g, b] = bank

        def scale_x(g, b):
            if b == 0:
                xg[g] = work.tile([P, TOK, PACK], BF16, name="xg", tag="xg", bufs=2, align_bytes=64)
            half = xg[g][:, HALF * b : HALF * (b + 1), :]
            scale = xs[:, g, :].rearrange("p (u e) -> p u e", e=2).unsqueeze(1)
            nc.vector.tensor_tensor(
                out=half.rearrange("p r (u e) -> p r u e", e=2),
                in0=xbank[g, b][:].bitcast(BF16).rearrange("p u l (r e) -> p (l r) u e", e=2),
                in1=scale.to_broadcast([P, HALF, 2, 2]),
                op=ALU.mult,
            )

        def quant_x(g):
            nc.vector.quantize_mx(
                out=xc[g][:].bitcast(FP8X4), scales=xcs[g][:], in_=xg[g][:].rearrange("p r t -> p (r t)")
            )

        acc = {}
        s_tile = {}

        def gate_mx(j, g):
            k, c = (0, j) if j < SWEEP else (1, j - SWEEP)
            if g == 0:
                acc[j] = psum.tile([P, TOK], F32, name="mx", tag="mx", bufs=SWEEP)
            nc.tensor.matmul_mx(
                out=acc[j][:],
                lhsT=wg[k][g][:, 2 * P * c : 2 * P * (c + 1)].bitcast(FP4X4),
                lhsT_scale=wgs[:, g, P * j : P * (j + 1)],
                rhs=xc[g][:].bitcast(FP8X4),
                rhs_scale=xcs[g][:],
                start=(g == 0),
                stop=(g == NP - 1),
            )

        def silu(j):
            s = work.tile([P, TOK], F32, name="s", tag="s", bufs=8)
            nc.scalar.activation(s[:], acc[j][:], ACT.Silu, bias=bg_col[:, j : j + 1])
            s_tile[j] = s

        def spread(j):
            nc.sync.dma_start(out=scratch[P * j : P * (j + 1), :], in_=s_tile[j][:])

        def fetch(g):
            rows = scratch[KP * g : KP * (g + 1), :]
            nc.sync.dma_start(out=sp[g][:], in_=rows.rearrange("(p t) n -> p t n", t=PACK))

        gh = {}
        gT = {}
        hb = {}

        def channels(g, q):
            return slice(KP * g + GRP * q, KP * g + GRP * (q + 1))

        def stats(i, g):
            def one(q):
                c = NJ * (i % 2) + 4 * g + q
                return lambda: nc.vector.bn_stats(out=st[i // 2][:, c, :], in_=at[i][:, channels(g, q)])
            return [one(q) for q in range(4)]

        def small(name):
            return work.tile([P, NC], F32, name=name, tag=name, bufs=2)

        def rsqrt_steps(h):
            me, m2e, mo, m2o = (st[h][:, :, f] for f in (1, 2, 4, 5))
            V = nc.vector
            d, v, q, sm = small("d"), small("v"), small("q"), small("sm")
            steps = [
                lambda: V.tensor_tensor(out=d[:], in0=me, in1=mo, op=ALU.subtract),
                lambda: V.scalar_tensor_tensor(out=v[:], in0=m2e, scalar=GRP * EPS, in1=m2o, op0=ALU.add, op1=ALU.add),
                lambda: V.scalar_tensor_tensor(out=q[:], in0=d[:], scalar=0.25, in1=d[:], op0=ALU.mult, op1=ALU.mult),
                lambda: V.tensor_tensor(out=sm[:], in0=me, in1=mo, op=ALU.add),
                lambda: V.scalar_tensor_tensor(
                    out=var[h][:], in0=v[:], scalar=1.0 / GRP, in1=q[:], op0=ALU.mult, op1=ALU.add
                ),
                lambda: V.tensor_scalar(
                    out=half_bits[h][:], in0=var[h][:].bitcast(I32), scalar1=1, scalar2=None, op0=ALU.arith_shift_right
                ),
                lambda: V.tensor_scalar(
                    out=y0[h][:], in0=half_bits[h][:], scalar1=-1.0, scalar2=RSQRT_MAGIC, op0=ALU.mult, op1=ALU.add
                ),
            ]

            def round(y, last):
                a, b = small("na"), small("nb")
                return [
                    lambda: V.tensor_tensor(out=a[:], in0=y, in1=y, op=ALU.mult),
                    lambda: V.scalar_tensor_tensor(
                        out=b[:], in0=a[:], scalar=-0.5, in1=var[h][:], op0=ALU.mult, op1=ALU.mult
                    ),
                    lambda: V.scalar_tensor_tensor(out=last, in0=b[:], scalar=1.5, in1=y, op0=ALU.add, op1=ALU.mult),
                ]

            y1, y2 = small("y1"), small("y2")
            steps += round(y0[h][:].bitcast(F32), y1[:]) + round(y1[:], y2[:]) + round(y2[:], rs[h][:])
            steps.append(
                lambda: V.scalar_tensor_tensor(
                    out=nmr[h][:], in0=sm[:], scalar=-0.5, in1=rs[h][:], op0=ALU.mult, op1=ALU.mult
                )
            )
            return steps

        def weave(main, side):
            for k, one in enumerate(main):
                one()
                if k < len(side):
                    side[k]()
            for one in side[len(main) :]:
                one()

        def norm(i, g, eng):
            t = work.tile([P, PACK, P], F32, name="gh", tag="gh", bufs=10)
            gh[i, g] = t

            def one(q):
                c = NJ * (i % 2) + 4 * g + q
                src = at[i][:, channels(g, q)].rearrange("p (m t) -> p t m", t=PACK)
                dst = t[:, :, 32 * q : 32 * (q + 1)]
                r, b = rs[i // 2][:, c : c + 1], nmr[i // 2][:, c : c + 1]
                if eng == "A":
                    return lambda: nc.scalar.activation(dst, src, ACT.Identity, bias=b, scale=r)
                return lambda: nc.vector.tensor_scalar(
                    out=dst, in0=src, scalar1=r, scalar2=b, op0=ALU.mult, op1=ALU.add
                )
            return [one(q) for q in range(4)]

        def norm_pair(h, g):
            for l in range(2):
                weave(norm(2 * h + l, g, "A"), [])

        tbank = {}

        def turn_g(h, g, tp):
            bank = psum.tile([P, 2, 2, P], F32, name="tr", tag="tr", bufs=2)
            for u in range(2):
                for l in range(2):
                    nc.tensor.transpose(bank[:, u, l, :], gh[2 * h + l, g][:, 2 * tp + u, :], ident[:])
            tbank[h, g, tp] = bank

        def affine(h, g, tp):
            if tp == 0:
                gT[h, g] = work.tile([P, PACK, HALF], F32, name="gT", tag="gT", bufs=3)
            for u in range(2):
                t = 2 * tp + u
                nc.scalar.activation(
                    gT[h, g][:, t, :], tbank[h, g, tp][:, u, :, :].rearrange("p l n -> p (l n)"), ACT.Identity,
                    bias=b_col[:, g, t : t + 1], scale=w_col[:, g, t : t + 1],
                )

        def gate_mul(h, g):
            hb[h, g] = work.tile([P, HALF, PACK], BF16, name="hb", tag="hb", bufs=3, align_bytes=64)
            nc.vector.tensor_tensor(
                out=hb[h, g][:].rearrange("p (c i) t -> p c t i", i=4),
                in0=gT[h, g][:].rearrange("p t (c i) -> p c t i", i=4),
                in1=sp[g][:, :, HALF * h : HALF * (h + 1)].rearrange("p t (c i) -> p c t i", i=4),
                op=ALU.mult,
            )

        def quant_h(h, g):
            nc.vector.quantize_mx(
                out=hc[h][g][:].bitcast(FP8X4), scales=hcs[h][g][:], in_=hb[h, g][:].rearrange("p r t -> p (r t)")
            )

        acc2 = {}

        def out_mx(h, k, g):
            l, n = divmod(k, 4)
            if g == 0:
                acc2[h, k] = psum.tile([P, TOK], F32, name="mx", tag="mx", bufs=SWEEP)
            nc.tensor.matmul_mx(
                out=acc2[h, k][:],
                lhsT=hc[h][g][:, P * l : P * (l + 1)].bitcast(FP8X4),
                lhsT_scale=hcs[h][g][:, P * l : P * (l + 1)],
                rhs=wo[g][:, 2 * KP * n : 2 * KP * (n + 1)].bitcast(FP4X4),
                rhs_scale=wos[:, g, KP * n : KP * (n + 1)],
                start=(g == 0),
                stop=(g == NP - 1),
            )

        bo_bank = {}

        def bo_mm(n):
            bo_bank[n] = psum.tile([P, KP], F32, name="mx", tag="mx", bufs=SWEEP)
            nc.tensor.matmul(bo_bank[n][:], lhsT=ones[:], rhs=bo_row[:, KP * n : KP * (n + 1)], start=True, stop=True)

        def bo_copy(n):
            nc.scalar.copy(out=bo_bc[:, KP * n : KP * (n + 1)], in_=bo_bank[n][:])

        bg_bank = {}

        def bg_turn():
            bg_bank[0] = psum.tile([P, TOK], F32, name="tr", tag="tr", bufs=2)
            nc.tensor.transpose(bg_bank[0][:, 0:P], bg_sq[:], ident[:])

        def bg_copy():
            nc.scalar.copy(out=bg_col[:], in_=bg_bank[0][:, 0:NJ])

        o_tile = {}

        def finish(h, k):
            n = k % 4
            o = work.tile([P, KP], F32, name="o", tag="o", bufs=6)
            nc.vector.tensor_tensor(
                out=o[:], in0=acc2[h, k][:], in1=bo_bc[:, KP * n : KP * (n + 1)], op=ALU.add
            )
            o_tile[h, k] = o

        def store(h, k):
            l, n = divmod(k, 4)
            i = 2 * h + l
            nc.sync.dma_start(out=out[0, P * i : P * (i + 1), KP * n : KP * (n + 1)], in_=o_tile[h, k][:])

        def gate_tiles(*js):
            for j in js:
                for g in range(NP):
                    gate_mx(j, g)

        def out_tile(h, k):
            for g in range(NP):
                out_mx(h, k, g)

        def emit(ops):
            weave(ops, [])

        steps = [rsqrt_steps(0), rsqrt_steps(1)]
        load_scales(wgs, Wg_scales)
        load_wg(0, 0)
        load_small()
        load_attn(0)
        load_wg(0, 1)
        load_wg(0, 2)
        load_attn(1)
        widen(0, 0, "V")
        widen(0, 2, "A")
        widen(0, 1, "V")
        widen(0, 3, "A")
        turn_x(0, 0)
        turn_x(0, 1)
        scale_x(0, 0)
        load_wg(0, 3)
        widen(1, 0, "A")
        widen(1, 1, "A")
        scale_x(0, 1)
        widen(1, 2, "A")
        turn_x(1, 0)
        widen(1, 3, "A")
        load_wg(1, 0)
        scale_x(1, 0)
        widen(2, 0, "A")
        load_wg(1, 1)
        turn_x(1, 1)
        load_wg(1, 2)
        widen(2, 1, "A")
        quant_x(0)
        widen(2, 2, "A")
        turn_x(2, 0)
        load_wg(1, 3)
        scale_x(1, 1)
        load_attn(2)
        widen(2, 3, "A")
        gate_mx(0, 0)
        load_attn(3)
        gate_mx(1, 0)
        widen(3, 0, "A")
        scale_x(2, 0)
        gate_mx(2, 0)
        gate_mx(3, 0)
        widen(3, 1, "A")
        turn_x(2, 1)
        load_scales(wos, Wo_scales)
        widen(3, 2, "A")
        quant_x(1)
        load_wo(0)
        turn_x(3, 0)
        widen(3, 3, "A")
        scale_x(2, 1)
        load_wo(1)
        gate_mx(4, 0)
        gate_mx(5, 0)
        gate_mx(0, 1)
        gate_mx(1, 1)
        scale_x(3, 0)
        gate_mx(2, 1)
        turn_x(3, 1)
        quant_x(2)
        bg_turn()
        gate_mx(3, 1)
        bg_copy()
        scale_x(3, 1)
        gate_mx(4, 1)
        gate_mx(5, 1)
        gate_mx(0, 2)
        gate_mx(1, 2)
        gate_mx(2, 2)
        quant_x(3)
        gate_mx(3, 2)
        gate_mx(4, 2)
        emit(stats(0, 0))
        gate_mx(5, 2)
        gate_mx(0, 3)
        gate_mx(1, 3)
        emit(stats(0, 1))
        silu(0)
        gate_mx(2, 3)
        gate_mx(3, 3)
        emit(stats(0, 2))
        silu(1)
        gate_mx(4, 3)
        spread(0)
        gate_mx(5, 3)
        silu(2)
        gate_tiles(6)
        emit(stats(0, 3))
        spread(1)
        silu(3)
        spread(2)
        emit(stats(1, 0))
        silu(4)
        bo_mm(0)
        spread(3)
        emit(stats(1, 1))
        bo_mm(1)
        silu(6)
        spread(4)
        gate_tiles(7)
        emit(stats(1, 2))
        silu(5)
        spread(6)
        emit(stats(1, 3))
        bo_copy(0)
        spread(5)
        load_wo(2)
        gate_tiles(8)
        silu(7)
        weave(stats(2, 0), steps[0][0:5])
        spread(7)
        bo_mm(2)
        silu(8)
        gate_tiles(9)
        weave(stats(2, 1), steps[0][5:9])
        bo_copy(1)
        spread(8)
        fetch(0)
        bo_copy(2)
        gate_tiles(10)
        weave(stats(2, 2), steps[0][9:13])
        silu(9)
        weave(stats(2, 3), steps[0][13:17])
        spread(9)
        gate_tiles(11)
        silu(10)
        emit(stats(3, 0))
        spread(10)
        emit(norm(0, 0, "A"))
        gate_tiles(12)
        emit(stats(3, 1))
        silu(11)
        emit(stats(3, 2))
        gate_tiles(13)
        emit(norm(1, 0, "A"))
        spread(11)
        fetch(1)
        emit(stats(3, 3))
        silu(12)
        turn_g(0, 0, 0)
        emit(norm(0, 1, "A"))
        spread(12)
        weave(norm(0, 2, "V"), steps[1][0:5])
        gate_tiles(14)
        affine(0, 0, 0)
        weave(norm(1, 2, "V"), steps[1][5:9])
        silu(13)
        gate_tiles(15)
        weave(norm(0, 3, "V"), steps[1][9:13])
        silu(14)
        spread(13)
        weave(norm(1, 3, "V"), steps[1][13:17])
        emit(norm(1, 1, "A"))
        spread(14)
        turn_g(0, 0, 1)
        bo_mm(3)
        silu(15)
        turn_g(0, 1, 0)
        affine(0, 0, 1)
        spread(15)
        fetch(2)
        load_wo(3)
        affine(0, 1, 0)
        gate_mul(0, 0)
        turn_g(0, 1, 1)
        affine(0, 1, 1)
        turn_g(0, 2, 0)
        affine(0, 2, 0)
        turn_g(0, 2, 1)
        quant_h(0, 0)
        gate_mul(0, 1)
        affine(0, 2, 1)
        turn_g(0, 3, 0)
        fetch(3)
        out_mx(0, 0, 0)
        bo_copy(3)
        out_mx(0, 1, 0)
        out_mx(0, 2, 0)
        affine(0, 3, 0)
        quant_h(0, 1)
        out_mx(0, 3, 0)
        out_mx(0, 4, 0)
        emit(norm(2, 0, "A"))
        out_mx(0, 5, 0)
        out_mx(0, 0, 1)
        emit(norm(3, 0, "A"))
        turn_g(0, 3, 1)
        gate_mul(0, 2)
        affine(0, 3, 1)
        turn_g(1, 0, 0)
        affine(1, 0, 0)
        turn_g(1, 0, 1)
        quant_h(0, 2)
        out_mx(0, 1, 1)
        affine(1, 0, 1)
        out_mx(0, 2, 1)
        out_mx(0, 3, 1)
        emit(norm(2, 1, "A"))
        out_mx(0, 4, 1)
        gate_mul(1, 0)
        out_mx(0, 5, 1)
        out_mx(0, 0, 2)
        emit(norm(3, 1, "A"))
        out_mx(0, 1, 2)
        out_mx(0, 2, 2)
        gate_mul(0, 3)
        emit(norm(2, 2, "A"))
        out_mx(0, 3, 2)
        turn_g(1, 1, 0)
        emit(norm(3, 2, "A"))
        turn_g(1, 1, 1)
        quant_h(1, 0)
        out_mx(0, 4, 2)
        quant_h(0, 3)
        affine(1, 1, 0)
        out_mx(0, 5, 2)
        out_mx(0, 0, 3)
        affine(1, 1, 1)
        out_mx(0, 1, 3)
        finish(0, 0)
        out_mx(0, 2, 3)
        out_mx(0, 3, 3)
        emit(norm(2, 3, "A"))
        finish(0, 1)
        out_mx(0, 4, 3)
        store(0, 0)
        turn_g(1, 2, 0)
        finish(0, 2)
        emit(norm(3, 3, "A"))
        store(0, 1)
        turn_g(1, 2, 1)
        finish(0, 3)
        store(0, 2)
        out_mx(0, 5, 3)
        affine(1, 2, 0)
        out_tile(0, 6)
        finish(0, 4)
        store(0, 3)
        affine(1, 2, 1)
        gate_mul(1, 1)
        store(0, 4)
        turn_g(1, 3, 0)
        turn_g(1, 3, 1)
        affine(1, 3, 0)
        finish(0, 5)
        out_tile(0, 7)
        affine(1, 3, 1)
        quant_h(1, 1)
        store(0, 5)
        finish(0, 6)
        out_mx(1, 0, 0)
        finish(0, 7)
        store(0, 6)
        out_mx(1, 1, 0)
        out_mx(1, 2, 0)
        gate_mul(1, 2)
        out_mx(1, 3, 0)
        store(0, 7)
        out_mx(1, 4, 0)
        out_mx(1, 5, 0)
        out_mx(1, 0, 1)
        out_mx(1, 1, 1)
        quant_h(1, 2)
        out_mx(1, 2, 1)
        out_mx(1, 3, 1)
        gate_mul(1, 3)
        out_mx(1, 4, 1)
        out_mx(1, 5, 1)
        out_mx(1, 0, 2)
        out_mx(1, 1, 2)
        out_mx(1, 2, 2)
        quant_h(1, 3)
        out_mx(1, 3, 2)
        out_mx(1, 4, 2)
        out_mx(1, 5, 2)
        out_mx(1, 0, 3)
        out_mx(1, 1, 3)
        finish(1, 0)
        out_mx(1, 2, 3)
        out_mx(1, 3, 3)
        finish(1, 1)
        out_mx(1, 4, 3)
        store(1, 0)
        out_mx(1, 5, 3)
        finish(1, 2)
        out_tile(1, 6)
        store(1, 1)
        finish(1, 3)
        store(1, 2)
        finish(1, 4)
        out_tile(1, 7)
        store(1, 3)
        finish(1, 5)
        store(1, 4)
        store(1, 5)
        finish(1, 6)
        finish(1, 7)
        store(1, 6)
        store(1, 7)
